import numpy as np
import ml_dtypes


def mxq(x, axis, fmt="e4m3"):
    dtype, down = {"e4m3": (ml_dtypes.float8_e4m3fn, 7), "e5m2": (ml_dtypes.float8_e5m2, 14)}[fmt]
    v = np.moveaxis(np.asarray(x, np.float32).astype(ml_dtypes.bfloat16).astype(np.float64), axis, -1)
    blocks = v.reshape(v.shape[:-1] + (-1, 32))
    amax = np.abs(blocks).max(-1, keepdims=True)
    byte = np.maximum(np.where(amax > 0, np.frexp(amax)[1] - 1 + 127, 0) - down, 1)
    scale = np.exp2(byte - 127.0)
    codes = (blocks / scale).astype(np.float32).astype(dtype).astype(np.float64)
    return np.moveaxis((codes * scale).reshape(v.shape), -1, axis)


WIDE = False


def mx_kscale(k):
    if not WIDE:
        return np.ones(k)
    levels = np.array([10, -10, 5, -5, 0])
    if k % 512:
        return np.exp2(np.random.permutation(np.resize(levels, k // 32))).repeat(32)
    a = np.empty((k // 512, 16))
    for p in range(k // 512):
        a[p, :8] = np.random.permutation(np.resize(levels, 8))
        for g in range(8):
            far = levels[np.abs(levels - a[p, g]) >= 10]
            a[p, g + 8] = far[np.random.randint(len(far))]
    return np.exp2(a.ravel()).repeat(32)


BF16 = ml_dtypes.bfloat16


def bf(x):
    return np.asarray(x, np.float32).astype(BF16)


def f64(x):
    return np.asarray(x).astype(np.float64)


B, S, H, HO, E = 4, 128, 1024, 1024, 8


def kahan_sum_last(x):
    s = np.zeros_like(x[..., 0])
    c = np.zeros_like(s)
    for i in range(x.shape[-1]):
        y = x[..., i] - c
        t = s + y
        c = (t - s) - y
        s = t
    return s


def setup_inputs():
    s = mx_kscale(H)
    return {"hidden_states": bf(np.random.standard_normal((B, S, H)) * s),
            "op_logits": bf(np.random.standard_normal((B, S, E)) * 1.3),
            "We": bf(np.random.standard_normal((E, H, HO)) / np.sqrt(H) / s[None, :, None]),
            "be": bf(np.random.standard_normal((E, HO)) * 0.3)}


def core(hidden_states, op_logits, We, be):
    l = f64(op_logits)
    ex = np.exp(l - l.max(-1, keepdims=True))
    op_w = ex / ex.sum(-1, keepdims=True)
    prod = mxq(f64(hidden_states), 2, "e4m3")[:, None] @ mxq(f64(We), 1, "e4m3")[None]
    expert_out = prod.transpose(0, 2, 1, 3) + f64(be)
    weighted = expert_out * op_w[:, :, :, None]
    return kahan_sum_last(np.moveaxis(weighted, 2, -1))


def e4m3fn_bytes(y):
    return np.clip(np.asarray(y, np.float64), -448.0, 448.0).astype(np.float32).astype(ml_dtypes.float8_e4m3fn).view(np.uint8)


Y_SCALE = 380.0


def reference(hidden_states, op_logits, We, be):
    out = core(hidden_states, op_logits, We, be)
    return out, e4m3fn_bytes(out * Y_SCALE)

@@ -1,0 +1,229 @@
+from contextlib import ExitStack
+
+import concourse.mybir as mybir
+from concourse.masks import make_identity
+
+FLOPS = 2 * 512 * 1024 * 1024 * 8
+
+F32 = mybir.dt.float32
+BF16 = mybir.dt.bfloat16
+U32 = mybir.dt.uint32
+U8 = mybir.dt.uint8
+FP8X4 = mybir.dt.float8_e4m3fn_x4
+FP8 = mybir.dt.float8_e4m3fn
+ALU = mybir.AluOpType
+ACT = mybir.ActivationFunctionType
+AX = mybir.AxisListType
+
+P = 128
+T = 4
+E = 8
+KDIM = 1024
+NDIM = 1024
+G = 2
+NW = 512
+UNITS = 16
+Y_SCALE = 380.0
+XG = 320
+XS = G * NW - XG
+Q_WIDTHS = (1024, 512, 256, 128, 64, 32)
+
+
+def tile_enhancedmathematicalreasoning_pa_kernel(tc, hidden_states, op_logits, We, be, out_0, out_1):
+    nc = tc.nc
+    with ExitStack() as ctx:
+        const = ctx.enter_context(tc.tile_pool(name="const", bufs=1))
+        grp = ctx.enter_context(tc.tile_pool(name="grp", bufs=3))
+        grg = ctx.enter_context(tc.tile_pool(name="grg", bufs=1))
+        cod = ctx.enter_context(tc.tile_pool(name="cod", bufs=3))
+        psum = ctx.enter_context(tc.psum_pool(name="psum", bufs=8))
+        ctx.enter_context(tc.manual_schedule())
+
+        lg = const.tile([P, T, E], BF16, name="lg")
+        raw = []
+        for e in range(E):
+            raw_e = const.tile([P, G, 4, NDIM], BF16, name="raw%d" % e)
+            raw.append(raw_e)
+        hraw = const.tile([P, T, KDIM], BF16, name="hraw")
+        be3 = const.tile([P, NDIM], BF16, name="be3")
+        hg = const.tile([P, T, KDIM], BF16, name="hg", align_bytes=64)
+        hc = const.tile([P, T, KDIM // 4], U32, name="hc", align_bytes=64)
+        hs = const.tile([P, T, KDIM // 4], U8, name="hs", align_bytes=64)
+        acc = const.tile([P, T, NDIM], F32, name="acc")
+        o8 = const.tile([P, T, NDIM], FP8, name="o8")
+        ident_f = const.tile([P, P], F32, name="ident_f")
+        ident_b = const.tile([P, P], BF16, name="ident_b")
+        wsp = const.tile([P, T, P], BF16, name="wsp")
+        wT = const.tile([P, T, P], BF16, name="wT")
+        warm = const.tile([P, 1], F32, name="warm")
+        warm2 = const.tile([P, 1], F32, name="warm2")
+        mx = const.tile([P, T], F32, name="mx")
+        nmx = const.tile([P, T], F32, name="nmx")
+        sm = const.tile([P, T], F32, name="sm")
+        rs = const.tile([P, T], F32, name="rs")
+        ex = const.tile([P, T, E], F32, name="ex")
+        w = const.tile([P, T, E], F32, name="w")
+        r1 = const.tile([P, T, E], F32, name="r1")
+        r2 = const.tile([P, T, E], F32, name="r2")
+
+        def load_w(e, g, n0, n1):
+            nc.sync.dma_start(
+                out=raw[e][:, g, :, n0:n1],
+                in_=We[e, g * 512 : (g + 1) * 512, n0:n1].rearrange("(p j) n -> p j n", j=4),
+            )
+
+        nc.vector.memset(warm[:], 0.0)
+        nc.scalar.activation(out=warm2[:], in_=warm[:], func=ACT.Exp)
+        nc.vector.memset(be3[:], 0.0)
+        nc.vector.memset(wsp[:], 0.0)
+        make_identity(nc, ident_b[:])
+        make_identity(nc, ident_f[:])
+
+        nc.sync.dma_start(out=lg[:], in_=op_logits.rearrange("b s e -> s b e"))
+        load_w(0, 0, 0, NW)
+        load_w(0, 1, 0, NW)
+        for r in range(3):
+            nc.sync.dma_start(out=be3[8 * r : 8 * r + 8, :], in_=be[:, :])
+        for t in range(T):
+            nc.sync.dma_start(out=hraw[:, t, :], in_=hidden_states[t, :, :])
+        load_w(0, 0, NW, NDIM)
+        load_w(0, 1, NW, NDIM)
+        for e in range(1, E):
+            for g in range(G):
+                load_w(e, g, 0, NDIM)
+
+        grouped_s = {}
+        grouped_g = {}
+        codes = {}
+        scales = {}
+        banks = {}
+
+        def rows_to_words(dst, src):
+            return dst.rearrange("p (c j) -> p c j", j=4), src.rearrange("p j c -> p c j")
+
+        def interleave(u):
+            e, n0 = u // 2, (u % 2) * NW
+            gs = grp.tile([P, 4 * XS], BF16, name="gs%d" % u, tag="gs", align_bytes=64)
+            gg = grg.tile([P, 4 * XG], BF16, name="gg%d" % u, tag="gg", align_bytes=64)
+            grouped_s[u] = gs
+            grouped_g[u] = gg
+            dst, src = rows_to_words(gs[:, 0 : 4 * NW], raw[e][:, 0, :, n0 : n0 + NW])
+            nc.scalar.copy(out=dst, in_=src)
+            dst, src = rows_to_words(gs[:, 4 * NW : 4 * XS], raw[e][:, 1, :, n0 : n0 + XS - NW])
+            nc.scalar.copy(out=dst, in_=src)
+            dst, src = rows_to_words(gg[:], raw[e][:, 1, :, n0 + XS - NW : n0 + NW])
+            nc.gpsimd.tensor_scalar(out=dst, in0=src, scalar1=1.0, scalar2=0.0, op0=ALU.mult, op1=ALU.add)
+
+        def quantize_region(src, ct, sc, x0, nx):
+            pos = 0
+            while pos < nx:
+                width = max([q for q in Q_WIDTHS if q <= nx - pos])
+                nc.vector.quantize_mx(
+                    out=ct[:, x0 + pos : x0 + pos + width].bitcast(FP8X4),
+                    scales=sc[:, x0 + pos : x0 + pos + width],
+                    in_=src[:, 4 * pos : 4 * (pos + width)],
+                )
+                pos += width
+
+        def quantize(u):
+            ct = cod.tile([P, G * NW], U32, name="ct%d" % u, tag="ct", align_bytes=64)
+            sc = cod.tile([P, G * NW], U8, name="sc%d" % u, tag="sc", align_bytes=64)
+            codes[u] = ct
+            scales[u] = sc
+            quantize_region(grouped_s[u], ct, sc, 0, XS)
+            quantize_region(grouped_g[u], ct, sc, XS, XG)
+
+        def multiply(u):
+            banks[u] = []
+            for t in range(T):
+                ps = psum.tile([P, NW], F32, name="ps%d_%d" % (u, t), tag="ps")
+                banks[u].append(ps)
+                for g in range(G):
+                    nc.tensor.matmul_mx(
+                        out=ps[:],
+                        lhsT=hc[:, t, g * P : (g + 1) * P].bitcast(FP8X4),
+                        lhsT_scale=hs[:, t, g * P : (g + 1) * P],
+                        rhs=codes[u][:, g * NW : (g + 1) * NW].bitcast(FP8X4),
+                        rhs_scale=scales[u][:, g * NW : (g + 1) * NW],
+                        start=(g == 0),
+                        stop=(g == G - 1),
+                    )
+
+        def accumulate(u):
+            e, nh = u // 2, u % 2
+            cols = slice(nh * NW, (nh + 1) * NW)
+            for t in range(T):
+                nc.vector.scalar_tensor_tensor(
+                    out=acc[:, t, cols], in0=banks[u][t][:], scalar=w[:, t, e : e + 1], in1=acc[:, t, cols],
+                    op0=ALU.mult, op1=ALU.add,
+                )
+                if e == E - 1:
+                    nc.sync.dma_start(out=out_0[t, :, cols], in_=acc[:, t, cols])
+                    nc.scalar.activation(
+                        out=o8[:, t, cols], in_=acc[:, t, cols], func=ACT.Copy, scale=Y_SCALE, saturate=False
+                    )
+                    nc.sync.dma_start(out=out_1[t, :, cols], in_=o8[:, t, cols].bitcast(U8))
+
+        nc.vector.tensor_reduce(out=mx[:], in_=lg[:], axis=AX.X, op=ALU.max)
+        nc.vector.tensor_scalar(out=nmx[:], in0=mx[:], scalar1=-1.0, scalar2=None, op0=ALU.mult)
+        for t in range(T):
+            nc.scalar.activation(
+                out=ex[:, t, :], in_=lg[:, t, :], func=ACT.Exp, bias=nmx[:, t : t + 1], scale=1.0,
+                accum_out=sm[:, t : t + 1],
+            )
+        interleave(0)
+        nc.vector.reciprocal(out=rs[:], in_=sm[:])
+        for t in range(T):
+            nc.vector.tensor_scalar(
+                out=w[:, t, :], in0=ex[:, t, :], scalar1=rs[:, t : t + 1], scalar2=None, op0=ALU.mult
+            )
+        nc.vector.tensor_copy(out=wsp[:, :, 0:8], in_=w[:])
+        nc.vector.tensor_tensor(out=r1[:], in0=w[:], in1=wsp[:, :, 0:8], op=ALU.subtract)
+        nc.vector.tensor_copy(out=wsp[:, :, 8:16], in_=r1[:])
+        nc.vector.tensor_tensor(out=r2[:], in0=r1[:], in1=wsp[:, :, 8:16], op=ALU.subtract)
+        nc.vector.tensor_copy(out=wsp[:, :, 16:24], in_=r2[:])
+        pw = psum.tile([P, T, P], BF16, name="pw", tag="ps")
+        for t in range(T):
+            nc.tensor.transpose(pw[:, t, :], wsp[:, t, :], ident_b[:])
+        nc.vector.tensor_copy(out=wT[:], in_=pw[:])
+
+        for t in range(T):
+            words = hraw[:, t, :].bitcast(F32)
+            xt = psum.tile([P, 4, P], F32, name="xt%d" % t, tag="ps")
+            for g in range(G):
+                for u in range(2):
+                    nc.tensor.transpose(
+                        xt[:, 2 * g + u, :], words[:, 256 * g + u : 256 * (g + 1) : 2], ident_f[:]
+                    )
+            nc.vector.tensor_copy(
+                out=hg[:, t, :].bitcast(F32).rearrange("p (g r u) -> p g r u", g=2, u=2),
+                in_=xt[:].rearrange("p (g u) r -> p g r u", u=2),
+            )
+
+        pbs = []
+        for nh in range(2):
+            for t in range(T):
+                pb = psum.tile([P, NW], F32, name="pb%d_%d" % (nh, t), tag="ps")
+                pbs.append(pb)
+                nc.tensor.matmul(
+                    out=pb[:], lhsT=wT[:, t, :], rhs=be3[:, nh * NW : (nh + 1) * NW], start=True, stop=True
+                )
+        for t in range(T):
+            nc.vector.quantize_mx(out=hc[:, t, :].bitcast(FP8X4), scales=hs[:, t, :], in_=hg[:, t, :])
+        for t in range(T):
+            nc.scalar.copy(out=acc[:, t, 0:NW], in_=pbs[t][:])
+        quantize(0)
+        multiply(0)
+        interleave(1)
+        for t in range(T):
+            nc.vector.tensor_copy(out=acc[:, t, NW:NDIM], in_=pbs[T + t][:])
+        quantize(1)
+        multiply(1)
+
+        for u in range(2, UNITS):
+            interleave(u)
+            accumulate(u - 2)
+            quantize(u)
+            multiply(u)
+        accumulate(UNITS - 2)
+        accumulate(UNITS - 1)

@@ -99,7 +99,7 @@ def tile_enhancedmathematicalreasoning_pa_kernel(tc, hidden_states, op_logits, W
         banks = {}
 
         def rows_to_words(dst, src):
-            return dst.rearrange("p (c j) -> p c j", j=4), src.rearrange("p j c -> p c j")
+            return dst.rearrange("p (c i j) -> p c j i", i=4, j=4), src.rearrange("p j (c i) -> p c j i", i=4)
 
         def interleave(u):
             e, n0 = u // 2, (u % 2) * NW

@@ -25,12 +25,11 @@ NW = 512
 UNITS = 16
 Y_SCALE = 380.0
 XG = 320
-XS = G * NW - XG
-Q_WIDTHS = (1024, 512, 256, 128, 64, 32)
 
 
 def tile_enhancedmathematicalreasoning_pa_kernel(tc, hidden_states, op_logits, We, be, out_0, out_1):
     nc = tc.nc
+    ORDER = [(e, nh) for e in range(6) for nh in range(2)] + [(6, 0), (7, 0), (6, 1), (7, 1)]
     with ExitStack() as ctx:
         const = ctx.enter_context(tc.tile_pool(name="const", bufs=1))
         grp = ctx.enter_context(tc.tile_pool(name="grp", bufs=3))
@@ -92,46 +91,39 @@ def tile_enhancedmathematicalreasoning_pa_kernel(tc, hidden_states, op_logits, W
             for g in range(G):
                 load_w(e, g, 0, NDIM)
 
-        grouped_s = {}
-        grouped_g = {}
+        pass0 = {}
+        pass1 = {}
         codes = {}
         scales = {}
         banks = {}
 
         def rows_to_words(dst, src):
-            return dst.rearrange("p (c i j) -> p c j i", i=4, j=4), src.rearrange("p j (c i) -> p c j i", i=4)
+            return dst.rearrange("p (c j) -> p c j", j=4), src.rearrange("p j c -> p c j")
 
-        def interleave(u):
-            e, n0 = u // 2, (u % 2) * NW
-            gs = grp.tile([P, 4 * XS], BF16, name="gs%d" % u, tag="gs", align_bytes=64)
-            gg = grg.tile([P, 4 * XG], BF16, name="gg%d" % u, tag="gg", align_bytes=64)
-            grouped_s[u] = gs
-            grouped_g[u] = gg
-            dst, src = rows_to_words(gs[:, 0 : 4 * NW], raw[e][:, 0, :, n0 : n0 + NW])
+        def interleave_pass0(u):
+            e, n0 = ORDER[u][0], ORDER[u][1] * NW
+            g0 = grp.tile([P, 4 * NW], BF16, name="g0_%d" % u, tag="g0", align_bytes=64)
+            pass0[u] = g0
+            dst, src = rows_to_words(g0[:], raw[e][:, 0, :, n0 : n0 + NW])
             nc.scalar.copy(out=dst, in_=src)
-            dst, src = rows_to_words(gs[:, 4 * NW : 4 * XS], raw[e][:, 1, :, n0 : n0 + XS - NW])
+
+        def interleave_pass1(u):
+            e, n0 = ORDER[u][0], ORDER[u][1] * NW
+            g1 = grg.tile([P, 4 * NW], BF16, name="g1_%d" % u, tag="g1", align_bytes=64)
+            pass1[u] = g1
+            split = NW - XG
+            dst, src = rows_to_words(g1[:, 0 : 4 * split], raw[e][:, 1, :, n0 : n0 + split])
             nc.scalar.copy(out=dst, in_=src)
-            dst, src = rows_to_words(gg[:], raw[e][:, 1, :, n0 + XS - NW : n0 + NW])
+            dst, src = rows_to_words(g1[:, 4 * split : 4 * NW], raw[e][:, 1, :, n0 + split : n0 + NW])
             nc.gpsimd.tensor_scalar(out=dst, in0=src, scalar1=1.0, scalar2=0.0, op0=ALU.mult, op1=ALU.add)
-
-        def quantize_region(src, ct, sc, x0, nx):
-            pos = 0
-            while pos < nx:
-                width = max([q for q in Q_WIDTHS if q <= nx - pos])
-                nc.vector.quantize_mx(
-                    out=ct[:, x0 + pos : x0 + pos + width].bitcast(FP8X4),
-                    scales=sc[:, x0 + pos : x0 + pos + width],
-                    in_=src[:, 4 * pos : 4 * (pos + width)],
-                )
-                pos += width
 
         def quantize(u):
             ct = cod.tile([P, G * NW], U32, name="ct%d" % u, tag="ct", align_bytes=64)
             sc = cod.tile([P, G * NW], U8, name="sc%d" % u, tag="sc", align_bytes=64)
             codes[u] = ct
             scales[u] = sc
-            quantize_region(grouped_s[u], ct, sc, 0, XS)
-            quantize_region(grouped_g[u], ct, sc, XS, XG)
+            nc.vector.quantize_mx(out=ct[:, 0:NW].bitcast(FP8X4), scales=sc[:, 0:NW], in_=pass0[u][:])
+            nc.vector.quantize_mx(out=ct[:, NW : 2 * NW].bitcast(FP8X4), scales=sc[:, NW : 2 * NW], in_=pass1[u][:])
 
         def multiply(u):
             banks[u] = []
@@ -150,7 +142,7 @@ def tile_enhancedmathematicalreasoning_pa_kernel(tc, hidden_states, op_logits, W
                     )
 
         def accumulate(u):
-            e, nh = u // 2, u % 2
+            e, nh = ORDER[u]
             cols = slice(nh * NW, (nh + 1) * NW)
             for t in range(T):
                 nc.vector.scalar_tensor_tensor(
@@ -171,7 +163,8 @@ def tile_enhancedmathematicalreasoning_pa_kernel(tc, hidden_states, op_logits, W
                 out=ex[:, t, :], in_=lg[:, t, :], func=ACT.Exp, bias=nmx[:, t : t + 1], scale=1.0,
                 accum_out=sm[:, t : t + 1],
             )
-        interleave(0)
+        interleave_pass0(0)
+        interleave_pass1(0)
         nc.vector.reciprocal(out=rs[:], in_=sm[:])
         for t in range(T):
             nc.vector.tensor_scalar(
@@ -208,20 +201,27 @@ def tile_enhancedmathematicalreasoning_pa_kernel(tc, hidden_states, op_logits, W
                 nc.tensor.matmul(
                     out=pb[:], lhsT=wT[:, t, :], rhs=be3[:, nh * NW : (nh + 1) * NW], start=True, stop=True
                 )
-        for t in range(T):
-            nc.vector.quantize_mx(out=hc[:, t, :].bitcast(FP8X4), scales=hs[:, t, :], in_=hg[:, t, :])
+        nc.vector.quantize_mx(
+            out=hc[:].rearrange("p t x -> p (t x)").bitcast(FP8X4),
+            scales=hs[:].rearrange("p t x -> p (t x)"),
+            in_=hg[:].rearrange("p t k -> p (t k)"),
+        )
         for t in range(T):
             nc.scalar.copy(out=acc[:, t, 0:NW], in_=pbs[t][:])
+        interleave_pass0(1)
         quantize(0)
         multiply(0)
-        interleave(1)
+        interleave_pass1(1)
         for t in range(T):
             nc.vector.tensor_copy(out=acc[:, t, NW:NDIM], in_=pbs[T + t][:])
+        interleave_pass0(2)
         quantize(1)
         multiply(1)
 
         for u in range(2, UNITS):
-            interleave(u)
+            interleave_pass1(u)
+            if u + 1 < UNITS:
+                interleave_pass0(u + 1)
             accumulate(u - 2)
             quantize(u)
             multiply(u)

@@ -24,6 +24,7 @@ G = 2
 NW = 512
 UNITS = 16
 Y_SCALE = 380.0
+XP = 256
 XG = 320
 
 
@@ -35,7 +36,8 @@ def tile_enhancedmathematicalreasoning_pa_kernel(tc, hidden_states, op_logits, W
         grp = ctx.enter_context(tc.tile_pool(name="grp", bufs=3))
         grg = ctx.enter_context(tc.tile_pool(name="grg", bufs=1))
         cod = ctx.enter_context(tc.tile_pool(name="cod", bufs=3))
-        psum = ctx.enter_context(tc.psum_pool(name="psum", bufs=8))
+        psum = ctx.enter_context(tc.psum_pool(name="psum", bufs=6))
+        psum_pi = ctx.enter_context(tc.psum_pool(name="psum_pi", bufs=2))
         ctx.enter_context(tc.manual_schedule())
 
         lg = const.tile([P, T, E], BF16, name="lg")
@@ -104,8 +106,19 @@ def tile_enhancedmathematicalreasoning_pa_kernel(tc, hidden_states, op_logits, W
             e, n0 = ORDER[u][0], ORDER[u][1] * NW
             g0 = grp.tile([P, 4 * NW], BF16, name="g0_%d" % u, tag="g0", align_bytes=64)
             pass0[u] = g0
-            dst, src = rows_to_words(g0[:], raw[e][:, 0, :, n0 : n0 + NW])
+            split = NW - XP
+            pi = psum_pi.tile([P, 4 * XP], BF16, name="pi%d" % u, tag="pi")
+            for c0 in range(0, XP, P):
+                nc.tensor.matmul(
+                    out=pi[:, 4 * c0 : 4 * (c0 + P)],
+                    lhsT=ident_b[:],
+                    rhs=raw[e][:, 0, :, n0 + split + c0 : n0 + split + c0 + P].rearrange("p j c -> p c j"),
+                    start=True,
+                    stop=True,
+                )
+            dst, src = rows_to_words(g0[:, 0 : 4 * split], raw[e][:, 0, :, n0 : n0 + split])
             nc.scalar.copy(out=dst, in_=src)
+            nc.scalar.copy(out=g0[:, 4 * split : 4 * NW], in_=pi[:])
 
         def interleave_pass1(u):
             e, n0 = ORDER[u][0], ORDER[u][1] * NW

@@ -24,7 +24,7 @@ G = 2
 NW = 512
 UNITS = 16
 Y_SCALE = 380.0
-XP = 256
+XP = 128
 XG = 320
 
 

@@ -66,6 +66,7 @@ def tile_enhancedmathematicalreasoning_pa_kernel(tc, hidden_states, op_logits, W
         w = const.tile([P, T, E], F32, name="w")
         r1 = const.tile([P, T, E], F32, name="r1")
         r2 = const.tile([P, T, E], F32, name="r2")
+        zz = const.tile([P, NW], BF16, name="zz")
 
         def load_w(e, g, n0, n1):
             nc.sync.dma_start(
@@ -75,6 +76,7 @@ def tile_enhancedmathematicalreasoning_pa_kernel(tc, hidden_states, op_logits, W
 
         nc.vector.memset(warm[:], 0.0)
         nc.scalar.activation(out=warm2[:], in_=warm[:], func=ACT.Exp)
+        nc.vector.memset(zz[:], 0.0)
         nc.vector.memset(be3[:], 0.0)
         nc.vector.memset(wsp[:], 0.0)
         make_identity(nc, ident_b[:])
@@ -169,6 +171,14 @@ def tile_enhancedmathematicalreasoning_pa_kernel(tc, hidden_states, op_logits, W
                     )
                     nc.sync.dma_start(out=out_1[t, :, cols], in_=o8[:, t, cols].bitcast(U8))
 
+        dm = psum.tile([P, NW], F32, name="dm", tag="ps")
+
+        def keep_busy(n, rhs):
+            for i in range(n):
+                nc.tensor.matmul(out=dm[:], lhsT=ident_b[:], rhs=rhs, start=True, stop=True)
+
+        keep_busy(4, zz[:])
+
         nc.vector.tensor_reduce(out=mx[:], in_=lg[:], axis=AX.X, op=ALU.max)
         nc.vector.tensor_scalar(out=nmx[:], in0=mx[:], scalar1=-1.0, scalar2=None, op0=ALU.mult)
         for t in range(T):
@@ -177,6 +187,7 @@ def tile_enhancedmathematicalreasoning_pa_kernel(tc, hidden_states, op_logits, W
                 accum_out=sm[:, t : t + 1],
             )
         interleave_pass0(0)
+        keep_busy(1, raw[0][:, 0, 0, 0:NW])
         interleave_pass1(0)
         nc.vector.reciprocal(out=rs[:], in_=sm[:])
         for t in range(T):
@@ -192,6 +203,7 @@ def tile_enhancedmathematicalreasoning_pa_kernel(tc, hidden_states, op_logits, W
         for t in range(T):
             nc.tensor.transpose(pw[:, t, :], wsp[:, t, :], ident_b[:])
         nc.vector.tensor_copy(out=wT[:], in_=pw[:])
+        keep_busy(1, raw[0][:, 1, 0, 0:NW])
 
         for t in range(T):
             words = hraw[:, t, :].bitcast(F32)

@@ -156,13 +156,14 @@ def tile_enhancedmathematicalreasoning_pa_kernel(tc, hidden_states, op_logits, W
                         stop=(g == G - 1),
                     )
 
-        def accumulate(u):
+        def accumulate_tile(u, t, pieces=1):
             e, nh = ORDER[u]
-            cols = slice(nh * NW, (nh + 1) * NW)
-            for t in range(T):
+            width = NW // pieces
+            for i in range(pieces):
+                cols = slice(nh * NW + i * width, nh * NW + (i + 1) * width)
                 nc.vector.scalar_tensor_tensor(
-                    out=acc[:, t, cols], in0=banks[u][t][:], scalar=w[:, t, e : e + 1], in1=acc[:, t, cols],
-                    op0=ALU.mult, op1=ALU.add,
+                    out=acc[:, t, cols], in0=banks[u][t][:, i * width : (i + 1) * width], scalar=w[:, t, e : e + 1],
+                    in1=acc[:, t, cols], op0=ALU.mult, op1=ALU.add,
                 )
                 if e == E - 1:
                     nc.sync.dma_start(out=out_0[t, :, cols], in_=acc[:, t, cols])
@@ -170,6 +171,10 @@ def tile_enhancedmathematicalreasoning_pa_kernel(tc, hidden_states, op_logits, W
                         out=o8[:, t, cols], in_=acc[:, t, cols], func=ACT.Copy, scale=Y_SCALE, saturate=False
                     )
                     nc.sync.dma_start(out=out_1[t, :, cols], in_=o8[:, t, cols].bitcast(U8))
+
+        def accumulate(u):
+            for t in range(T):
+                accumulate_tile(u, t)
 
         dm = psum.tile([P, NW], F32, name="dm", tag="ps")
 
@@ -250,5 +255,16 @@ def tile_enhancedmathematicalreasoning_pa_kernel(tc, hidden_states, op_logits, W
             accumulate(u - 2)
             quantize(u)
             multiply(u)
-        accumulate(UNITS - 2)
-        accumulate(UNITS - 1)
+        a, b = UNITS - 2, UNITS - 1
+        e_a, nh_a = ORDER[a]
+        side = grg.tile([P, NW], F32, name="side", tag="g1", align_bytes=64)
+        nc.scalar.activation(out=side[:], in_=banks[a][T - 1][:], func=ACT.Copy, scale=w[:, T - 1, e_a : e_a + 1])
+        last_cols = slice(nh_a * NW, (nh_a + 1) * NW)
+        nc.gpsimd.tensor_tensor(out=acc[:, T - 1, last_cols], in0=acc[:, T - 1, last_cols], in1=side[:], op=ALU.add)
+        accumulate_tile(a, 0)
+        accumulate_tile(a, 1)
+        accumulate_tile(b, 0)
+        accumulate_tile(a, 2)
+        accumulate_tile(b, 1)
+        accumulate_tile(b, 2)
+        accumulate_tile(b, 3, pieces=2)

@@ -25,6 +25,7 @@ NW = 512
 UNITS = 16
 Y_SCALE = 380.0
 XP = 128
+XS = 2
 XG = 320
 
 
@@ -132,13 +133,21 @@ def tile_enhancedmathematicalreasoning_pa_kernel(tc, hidden_states, op_logits, W
             dst, src = rows_to_words(g1[:, 4 * split : 4 * NW], raw[e][:, 1, :, n0 + split : n0 + NW])
             nc.gpsimd.tensor_scalar(out=dst, in0=src, scalar1=1.0, scalar2=0.0, op0=ALU.mult, op1=ALU.add)
 
-        def quantize(u):
+        def quantize_pass0(u):
             ct = cod.tile([P, G * NW], U32, name="ct%d" % u, tag="ct", align_bytes=64)
             sc = cod.tile([P, G * NW], U8, name="sc%d" % u, tag="sc", align_bytes=64)
             codes[u] = ct
             scales[u] = sc
             nc.vector.quantize_mx(out=ct[:, 0:NW].bitcast(FP8X4), scales=sc[:, 0:NW], in_=pass0[u][:])
-            nc.vector.quantize_mx(out=ct[:, NW : 2 * NW].bitcast(FP8X4), scales=sc[:, NW : 2 * NW], in_=pass1[u][:])
+
+        def quantize_pass1(u):
+            nc.vector.quantize_mx(
+                out=codes[u][:, NW : 2 * NW].bitcast(FP8X4), scales=scales[u][:, NW : 2 * NW], in_=pass1[u][:]
+            )
+
+        def quantize(u):
+            quantize_pass0(u)
+            quantize_pass1(u)
 
         def multiply(u):
             banks[u] = []
@@ -218,7 +227,10 @@ def tile_enhancedmathematicalreasoning_pa_kernel(tc, hidden_states, op_logits, W
                     nc.tensor.transpose(
                         xt[:, 2 * g + u, :], words[:, 256 * g + u : 256 * (g + 1) : 2], ident_f[:]
                     )
-            nc.vector.tensor_copy(
+            if t == XS:
+                quantize_pass0(0)
+            copy_out = nc.scalar.copy if t < XS else nc.vector.tensor_copy
+            copy_out(
                 out=hg[:, t, :].bitcast(F32).rearrange("p (g r u) -> p g r u", g=2, u=2),
                 in_=xt[:].rearrange("p (g u) r -> p g r u", u=2),
             )
@@ -231,15 +243,16 @@ def tile_enhancedmathematicalreasoning_pa_kernel(tc, hidden_states, op_logits, W
                 nc.tensor.matmul(
                     out=pb[:], lhsT=wT[:, t, :], rhs=be3[:, nh * NW : (nh + 1) * NW], start=True, stop=True
                 )
+        quantize_pass1(0)
         nc.vector.quantize_mx(
             out=hc[:].rearrange("p t x -> p (t x)").bitcast(FP8X4),
             scales=hs[:].rearrange("p t x -> p (t x)"),
             in_=hg[:].rearrange("p t k -> p (t k)"),
         )
-        for t in range(T):
+        for t in range(T - 1):
             nc.scalar.copy(out=acc[:, t, 0:NW], in_=pbs[t][:])
+        nc.vector.tensor_copy(out=acc[:, T - 1, 0:NW], in_=pbs[T - 1][:])
         interleave_pass0(1)
-        quantize(0)
         multiply(0)
         interleave_pass1(1)
         for t in range(T):

@@ -25,7 +25,8 @@ NW = 512
 UNITS = 16
 Y_SCALE = 380.0
 XP = 128
-XS = 2
+XG1 = 160
+XS = 3
 XG = 320
 
 
@@ -105,7 +106,7 @@ def tile_enhancedmathematicalreasoning_pa_kernel(tc, hidden_states, op_logits, W
         def rows_to_words(dst, src):
             return dst.rearrange("p (c j) -> p c j", j=4), src.rearrange("p j c -> p c j")
 
-        def interleave_pass0(u):
+        def interleave_pass0(u, gpsimd_cols=0):
             e, n0 = ORDER[u][0], ORDER[u][1] * NW
             g0 = grp.tile([P, 4 * NW], BF16, name="g0_%d" % u, tag="g0", align_bytes=64)
             pass0[u] = g0
@@ -119,9 +120,16 @@ def tile_enhancedmathematicalreasoning_pa_kernel(tc, hidden_states, op_logits, W
                     start=True,
                     stop=True,
                 )
-            dst, src = rows_to_words(g0[:, 0 : 4 * split], raw[e][:, 0, :, n0 : n0 + split])
+            mine = split - gpsimd_cols
+            dst, src = rows_to_words(g0[:, 0 : 4 * mine], raw[e][:, 0, :, n0 : n0 + mine])
             nc.scalar.copy(out=dst, in_=src)
             nc.scalar.copy(out=g0[:, 4 * split : 4 * NW], in_=pi[:])
+
+        def interleave_pass0_gpsimd(u, gpsimd_cols):
+            e, n0 = ORDER[u][0], ORDER[u][1] * NW
+            c0, c1 = NW - XP - gpsimd_cols, NW - XP
+            dst, src = rows_to_words(pass0[u][:, 4 * c0 : 4 * c1], raw[e][:, 0, :, n0 + c0 : n0 + c1])
+            nc.gpsimd.tensor_scalar(out=dst, in0=src, scalar1=1.0, scalar2=0.0, op0=ALU.mult, op1=ALU.add)
 
         def interleave_pass1(u):
             e, n0 = ORDER[u][0], ORDER[u][1] * NW
@@ -219,6 +227,13 @@ def tile_enhancedmathematicalreasoning_pa_kernel(tc, hidden_states, op_logits, W
         nc.vector.tensor_copy(out=wT[:], in_=pw[:])
         keep_busy(1, raw[0][:, 1, 0, 0:NW])
 
+        def quantize_hidden(t0, t1):
+            nc.vector.quantize_mx(
+                out=hc[:, t0:t1, :].rearrange("p t x -> p (t x)").bitcast(FP8X4),
+                scales=hs[:, t0:t1, :].rearrange("p t x -> p (t x)"),
+                in_=hg[:, t0:t1, :].rearrange("p t k -> p (t k)"),
+            )
+
         for t in range(T):
             words = hraw[:, t, :].bitcast(F32)
             xt = psum.tile([P, 4, P], F32, name="xt%d" % t, tag="ps")
@@ -228,7 +243,8 @@ def tile_enhancedmathematicalreasoning_pa_kernel(tc, hidden_states, op_logits, W
                         xt[:, 2 * g + u, :], words[:, 256 * g + u : 256 * (g + 1) : 2], ident_f[:]
                     )
             if t == XS:
-                quantize_pass0(0)
+                quantize(0)
+                quantize_hidden(0, 2)
             copy_out = nc.scalar.copy if t < XS else nc.vector.tensor_copy
             copy_out(
                 out=hg[:, t, :].bitcast(F32).rearrange("p (g r u) -> p g r u", g=2, u=2),
@@ -243,18 +259,15 @@ def tile_enhancedmathematicalreasoning_pa_kernel(tc, hidden_states, op_logits, W
                 nc.tensor.matmul(
                     out=pb[:], lhsT=wT[:, t, :], rhs=be3[:, nh * NW : (nh + 1) * NW], start=True, stop=True
                 )
-        quantize_pass1(0)
-        nc.vector.quantize_mx(
-            out=hc[:].rearrange("p t x -> p (t x)").bitcast(FP8X4),
-            scales=hs[:].rearrange("p t x -> p (t x)"),
-            in_=hg[:].rearrange("p t k -> p (t k)"),
-        )
+        quantize_hidden(2, 3)
+        quantize_hidden(3, 4)
         for t in range(T - 1):
             nc.scalar.copy(out=acc[:, t, 0:NW], in_=pbs[t][:])
         nc.vector.tensor_copy(out=acc[:, T - 1, 0:NW], in_=pbs[T - 1][:])
-        interleave_pass0(1)
+        interleave_pass0(1, gpsimd_cols=XG1)
         multiply(0)
         interleave_pass1(1)
+        interleave_pass0_gpsimd(1, XG1)
         for t in range(T):
             nc.vector.tensor_copy(out=acc[:, t, NW:NDIM], in_=pbs[T + t][:])
         interleave_pass0(2)

@@ -61,13 +61,12 @@ def tile_enhancedmathematicalreasoning_pa_kernel(tc, hidden_states, op_logits, W
         warm = const.tile([P, 1], F32, name="warm")
         warm2 = const.tile([P, 1], F32, name="warm2")
         mx = const.tile([P, T], F32, name="mx")
-        nmx = const.tile([P, T], F32, name="nmx")
+        dl = const.tile([P, T, E], F32, name="dl")
         sm = const.tile([P, T], F32, name="sm")
         rs = const.tile([P, T], F32, name="rs")
         ex = const.tile([P, T, E], F32, name="ex")
         w = const.tile([P, T, E], F32, name="w")
         r1 = const.tile([P, T, E], F32, name="r1")
-        r2 = const.tile([P, T, E], F32, name="r2")
         zz = const.tile([P, NW], BF16, name="zz")
 
         def load_w(e, g, n0, n1):
@@ -87,7 +86,7 @@ def tile_enhancedmathematicalreasoning_pa_kernel(tc, hidden_states, op_logits, W
         nc.sync.dma_start(out=lg[:], in_=op_logits.rearrange("b s e -> s b e"))
         load_w(0, 0, 0, NW)
         load_w(0, 1, 0, NW)
-        for r in range(3):
+        for r in range(2):
             nc.sync.dma_start(out=be3[8 * r : 8 * r + 8, :], in_=be[:, :])
         for t in range(T):
             nc.sync.dma_start(out=hraw[:, t, :], in_=hidden_states[t, :, :])
@@ -202,25 +201,17 @@ def tile_enhancedmathematicalreasoning_pa_kernel(tc, hidden_states, op_logits, W
         keep_busy(4, zz[:])
 
         nc.vector.tensor_reduce(out=mx[:], in_=lg[:], axis=AX.X, op=ALU.max)
-        nc.vector.tensor_scalar(out=nmx[:], in0=mx[:], scalar1=-1.0, scalar2=None, op0=ALU.mult)
-        for t in range(T):
-            nc.scalar.activation(
-                out=ex[:, t, :], in_=lg[:, t, :], func=ACT.Exp, bias=nmx[:, t : t + 1], scale=1.0,
-                accum_out=sm[:, t : t + 1],
-            )
+        nc.vector.tensor_tensor(out=dl[:], in0=lg[:], in1=mx[:].unsqueeze(2).to_broadcast([P, T, E]), op=ALU.subtract)
+        nc.scalar.activation(out=ex[:], in_=dl[:], func=ACT.Exp)
         interleave_pass0(0)
         keep_busy(1, raw[0][:, 0, 0, 0:NW])
         interleave_pass1(0)
+        nc.vector.tensor_copy(out=wsp[:, :, 0:8], in_=ex[:])
+        nc.vector.tensor_reduce(out=sm[:], in_=ex[:], axis=AX.X, op=ALU.add)
+        nc.vector.tensor_tensor(out=r1[:], in0=ex[:], in1=wsp[:, :, 0:8], op=ALU.subtract)
         nc.vector.reciprocal(out=rs[:], in_=sm[:])
-        for t in range(T):
-            nc.vector.tensor_scalar(
-                out=w[:, t, :], in0=ex[:, t, :], scalar1=rs[:, t : t + 1], scalar2=None, op0=ALU.mult
-            )
-        nc.vector.tensor_copy(out=wsp[:, :, 0:8], in_=w[:])
-        nc.vector.tensor_tensor(out=r1[:], in0=w[:], in1=wsp[:, :, 0:8], op=ALU.subtract)
         nc.vector.tensor_copy(out=wsp[:, :, 8:16], in_=r1[:])
-        nc.vector.tensor_tensor(out=r2[:], in0=r1[:], in1=wsp[:, :, 8:16], op=ALU.subtract)
-        nc.vector.tensor_copy(out=wsp[:, :, 16:24], in_=r2[:])
+        nc.vector.tensor_tensor(out=w[:], in0=ex[:], in1=rs[:].unsqueeze(2).to_broadcast([P, T, E]), op=ALU.mult)
         pw = psum.tile([P, T, P], BF16, name="pw", tag="ps")
         for t in range(T):
             nc.tensor.transpose(pw[:, t, :], wsp[:, t, :], ident_b[:])
@@ -262,14 +253,18 @@ def tile_enhancedmathematicalreasoning_pa_kernel(tc, hidden_states, op_logits, W
         quantize_hidden(2, 3)
         quantize_hidden(3, 4)
         for t in range(T - 1):
-            nc.scalar.copy(out=acc[:, t, 0:NW], in_=pbs[t][:])
-        nc.vector.tensor_copy(out=acc[:, T - 1, 0:NW], in_=pbs[T - 1][:])
+            nc.scalar.activation(out=acc[:, t, 0:NW], in_=pbs[t][:], func=ACT.Copy, scale=rs[:, t : t + 1])
+        nc.vector.tensor_scalar(
+            out=acc[:, T - 1, 0:NW], in0=pbs[T - 1][:], scalar1=rs[:, T - 1 : T], scalar2=None, op0=ALU.mult
+        )
         interleave_pass0(1, gpsimd_cols=XG1)
         multiply(0)
         interleave_pass1(1)
         interleave_pass0_gpsimd(1, XG1)
         for t in range(T):
-            nc.vector.tensor_copy(out=acc[:, t, NW:NDIM], in_=pbs[T + t][:])
+            nc.vector.tensor_scalar(
+                out=acc[:, t, NW:NDIM], in0=pbs[T + t][:], scalar1=rs[:, t : t + 1], scalar2=None, op0=ALU.mult
+            )
         interleave_pass0(2)
         quantize(1)
         multiply(1)

@@ -198,13 +198,13 @@ def tile_enhancedmathematicalreasoning_pa_kernel(tc, hidden_states, op_logits, W
             for i in range(n):
                 nc.tensor.matmul(out=dm[:], lhsT=ident_b[:], rhs=rhs, start=True, stop=True)
 
-        keep_busy(4, zz[:])
+        keep_busy(7, zz[:])
 
         nc.vector.tensor_reduce(out=mx[:], in_=lg[:], axis=AX.X, op=ALU.max)
         nc.vector.tensor_tensor(out=dl[:], in0=lg[:], in1=mx[:].unsqueeze(2).to_broadcast([P, T, E]), op=ALU.subtract)
         nc.scalar.activation(out=ex[:], in_=dl[:], func=ACT.Exp)
         interleave_pass0(0)
-        keep_busy(1, raw[0][:, 0, 0, 0:NW])
+        keep_busy(2, raw[0][:, 0, 0, 0:NW])
         interleave_pass1(0)
         nc.vector.tensor_copy(out=wsp[:, :, 0:8], in_=ex[:])
         nc.vector.tensor_reduce(out=sm[:], in_=ex[:], axis=AX.X, op=ALU.add)
@@ -216,7 +216,7 @@ def tile_enhancedmathematicalreasoning_pa_kernel(tc, hidden_states, op_logits, W
         for t in range(T):
             nc.tensor.transpose(pw[:, t, :], wsp[:, t, :], ident_b[:])
         nc.vector.tensor_copy(out=wT[:], in_=pw[:])
-        keep_busy(1, raw[0][:, 1, 0, 0:NW])
+        keep_busy(2, raw[0][:, 1, 0, 0:NW])
 
         def quantize_hidden(t0, t1):
             nc.vector.quantize_mx(

@@ -92,7 +92,10 @@ def tile_enhancedmathematicalreasoning_pa_kernel(tc, hidden_states, op_logits, W
             nc.sync.dma_start(out=hraw[:, t, :], in_=hidden_states[t, :, :])
         load_w(0, 0, NW, NDIM)
         load_w(0, 1, NW, NDIM)
-        for e in range(1, E):
+        for n0 in (0, NW):
+            for g in range(G):
+                load_w(1, g, n0, n0 + NW)
+        for e in range(2, E):
             for g in range(G):
                 load_w(e, g, 0, NDIM)
 
@@ -139,6 +142,13 @@ def tile_enhancedmathematicalreasoning_pa_kernel(tc, hidden_states, op_logits, W
             nc.scalar.copy(out=dst, in_=src)
             dst, src = rows_to_words(g1[:, 4 * split : 4 * NW], raw[e][:, 1, :, n0 + split : n0 + NW])
             nc.gpsimd.tensor_scalar(out=dst, in0=src, scalar1=1.0, scalar2=0.0, op0=ALU.mult, op1=ALU.add)
+
+        def interleave_pass1_vector(u):
+            e, n0 = ORDER[u][0], ORDER[u][1] * NW
+            g1 = grg.tile([P, 4 * NW], BF16, name="g1_%d" % u, tag="g1", align_bytes=64)
+            pass1[u] = g1
+            dst, src = rows_to_words(g1[:], raw[e][:, 1, :, n0 : n0 + NW])
+            nc.vector.tensor_copy(out=dst, in_=src)
 
         def quantize_pass0(u):
             ct = cod.tile([P, G * NW], U32, name="ct%d" % u, tag="ct", align_bytes=64)
@@ -205,13 +215,13 @@ def tile_enhancedmathematicalreasoning_pa_kernel(tc, hidden_states, op_logits, W
         nc.scalar.activation(out=ex[:], in_=dl[:], func=ACT.Exp)
         interleave_pass0(0)
         keep_busy(2, raw[0][:, 0, 0, 0:NW])
-        interleave_pass1(0)
         nc.vector.tensor_copy(out=wsp[:, :, 0:8], in_=ex[:])
         nc.vector.tensor_reduce(out=sm[:], in_=ex[:], axis=AX.X, op=ALU.add)
         nc.vector.tensor_tensor(out=r1[:], in0=ex[:], in1=wsp[:, :, 0:8], op=ALU.subtract)
         nc.vector.reciprocal(out=rs[:], in_=sm[:])
         nc.vector.tensor_copy(out=wsp[:, :, 8:16], in_=r1[:])
         nc.vector.tensor_tensor(out=w[:], in0=ex[:], in1=rs[:].unsqueeze(2).to_broadcast([P, T, E]), op=ALU.mult)
+        interleave_pass1_vector(0)
         pw = psum.tile([P, T, P], BF16, name="pw", tag="ps")
         for t in range(T):
             nc.tensor.transpose(pw[:, t, :], wsp[:, t, :], ident_b[:])
@@ -242,14 +252,13 @@ def tile_enhancedmathematicalreasoning_pa_kernel(tc, hidden_states, op_logits, W
                 in_=xt[:].rearrange("p (g u) r -> p g r u", u=2),
             )
 
-        pbs = []
-        for nh in range(2):
-            for t in range(T):
-                pb = psum.tile([P, NW], F32, name="pb%d_%d" % (nh, t), tag="ps")
-                pbs.append(pb)
-                nc.tensor.matmul(
-                    out=pb[:], lhsT=wT[:, t, :], rhs=be3[:, nh * NW : (nh + 1) * NW], start=True, stop=True
-                )
+        pbs = {}
+        for nh, t in [(0, 0), (0, 3), (0, 1), (1, 0), (0, 2), (1, 1), (1, 2), (1, 3)]:
+            pb = psum.tile([P, NW], F32, name="pb%d_%d" % (nh, t), tag="ps")
+            pbs[T * nh + t] = pb
+            nc.tensor.matmul(
+                out=pb[:], lhsT=wT[:, t, :], rhs=be3[:, nh * NW : (nh + 1) * NW], start=True, stop=True
+            )
         quantize_hidden(2, 3)
         quantize_hidden(3, 4)
         for t in range(T - 1):

@@ -37,6 +37,7 @@ def tile_enhancedmathematicalreasoning_pa_kernel(tc, hidden_states, op_logits, W
         const = ctx.enter_context(tc.tile_pool(name="const", bufs=1))
         grp = ctx.enter_context(tc.tile_pool(name="grp", bufs=3))
         grg = ctx.enter_context(tc.tile_pool(name="grg", bufs=1))
+        grh = ctx.enter_context(tc.tile_pool(name="grh", bufs=1))
         cod = ctx.enter_context(tc.tile_pool(name="cod", bufs=3))
         psum = ctx.enter_context(tc.psum_pool(name="psum", bufs=6))
         psum_pi = ctx.enter_context(tc.psum_pool(name="psum_pi", bufs=2))
@@ -135,7 +136,8 @@ def tile_enhancedmathematicalreasoning_pa_kernel(tc, hidden_states, op_logits, W
 
         def interleave_pass1(u):
             e, n0 = ORDER[u][0], ORDER[u][1] * NW
-            g1 = grg.tile([P, 4 * NW], BF16, name="g1_%d" % u, tag="g1", align_bytes=64)
+            pool = grg if u < 2 else grh
+            g1 = pool.tile([P, 4 * NW], BF16, name="g1_%d" % u, tag="g1", align_bytes=64)
             pass1[u] = g1
             split = NW - XG
             dst, src = rows_to_words(g1[:, 0 : 4 * split], raw[e][:, 1, :, n0 : n0 + split])
@@ -275,10 +277,15 @@ def tile_enhancedmathematicalreasoning_pa_kernel(tc, hidden_states, op_logits, W
                 out=acc[:, t, NW:NDIM], in0=pbs[T + t][:], scalar1=rs[:, t : t + 1], scalar2=None, op0=ALU.mult
             )
         interleave_pass0(2)
+        interleave_pass1(2)
+        interleave_pass0(3)
+        accumulate(0)
         quantize(1)
         multiply(1)
+        quantize(2)
+        multiply(2)
 
-        for u in range(2, UNITS):
+        for u in range(3, UNITS):
             interleave_pass1(u)
             if u + 1 < UNITS:
                 interleave_pass0(u + 1)
@@ -287,7 +294,7 @@ def tile_enhancedmathematicalreasoning_pa_kernel(tc, hidden_states, op_logits, W
             multiply(u)
         a, b = UNITS - 2, UNITS - 1
         e_a, nh_a = ORDER[a]
-        side = grg.tile([P, NW], F32, name="side", tag="g1", align_bytes=64)
+        side = grh.tile([P, NW], F32, name="side", tag="g1", align_bytes=64)
         nc.scalar.activation(out=side[:], in_=banks[a][T - 1][:], func=ACT.Copy, scale=w[:, T - 1, e_a : e_a + 1])
         last_cols = slice(nh_a * NW, (nh_a + 1) * NW)
         nc.gpsimd.tensor_tensor(out=acc[:, T - 1, last_cols], in0=acc[:, T - 1, last_cols], in1=side[:], op=ALU.add)

@@ -32,6 +32,10 @@ XG = 320
 
 def tile_enhancedmathematicalreasoning_pa_kernel(tc, hidden_states, op_logits, We, be, out_0, out_1):
     nc = tc.nc
+    tokens_h = hidden_states.flatten_outer_dims().rearrange("(p t) k -> p t k", t=T)
+    tokens_l = op_logits.flatten_outer_dims().rearrange("(p t) e -> p t e", t=T)
+    tokens_0 = out_0.flatten_outer_dims().rearrange("(p t) n -> p t n", t=T)
+    tokens_1 = out_1.flatten_outer_dims().rearrange("(p t) n -> p t n", t=T)
     ORDER = [(e, nh) for e in range(6) for nh in range(2)] + [(6, 0), (7, 0), (6, 1), (7, 1)]
     with ExitStack() as ctx:
         const = ctx.enter_context(tc.tile_pool(name="const", bufs=1))
@@ -76,21 +80,21 @@ def tile_enhancedmathematicalreasoning_pa_kernel(tc, hidden_states, op_logits, W
                 in_=We[e, g * 512 : (g + 1) * 512, n0:n1].rearrange("(p j) n -> p j n", j=4),
             )
 
+        nc.scalar.dma_start(out=lg[:], in_=tokens_l)
         nc.vector.memset(warm[:], 0.0)
-        nc.scalar.activation(out=warm2[:], in_=warm[:], func=ACT.Exp)
-        nc.vector.memset(zz[:], 0.0)
         nc.vector.memset(be3[:], 0.0)
+        nc.scalar.activation(out=warm2[:], in_=warm[:], func=ACT.Exp)
+        for r in range(2):
+            nc.scalar.dma_start(out=be3[8 * r : 8 * r + 8, :], in_=be[:, :])
+        nc.vector.memset(zz[:], 0.0)
         nc.vector.memset(wsp[:], 0.0)
         make_identity(nc, ident_b[:])
         make_identity(nc, ident_f[:])
 
-        nc.sync.dma_start(out=lg[:], in_=op_logits.rearrange("b s e -> s b e"))
         load_w(0, 0, 0, NW)
         load_w(0, 1, 0, NW)
-        for r in range(2):
-            nc.sync.dma_start(out=be3[8 * r : 8 * r + 8, :], in_=be[:, :])
         for t in range(T):
-            nc.sync.dma_start(out=hraw[:, t, :], in_=hidden_states[t, :, :])
+            nc.sync.dma_start(out=hraw[:, t, :], in_=tokens_h[:, t, :])
         load_w(0, 0, NW, NDIM)
         load_w(0, 1, NW, NDIM)
         for n0 in (0, NW):
@@ -194,11 +198,11 @@ def tile_enhancedmathematicalreasoning_pa_kernel(tc, hidden_states, op_logits, W
                     in1=acc[:, t, cols], op0=ALU.mult, op1=ALU.add,
                 )
                 if e == E - 1:
-                    nc.sync.dma_start(out=out_0[t, :, cols], in_=acc[:, t, cols])
+                    nc.sync.dma_start(out=tokens_0[:, t, cols], in_=acc[:, t, cols])
                     nc.scalar.activation(
                         out=o8[:, t, cols], in_=acc[:, t, cols], func=ACT.Copy, scale=Y_SCALE, saturate=False
                     )
-                    nc.sync.dma_start(out=out_1[t, :, cols], in_=o8[:, t, cols].bitcast(U8))
+                    nc.sync.dma_start(out=tokens_1[:, t, cols], in_=o8[:, t, cols].bitcast(U8))
 
         def accumulate(u):
             for t in range(T):

@@ -82,11 +82,11 @@ def tile_enhancedmathematicalreasoning_pa_kernel(tc, hidden_states, op_logits, W
 
         nc.scalar.dma_start(out=lg[:], in_=tokens_l)
         nc.vector.memset(warm[:], 0.0)
-        nc.vector.memset(be3[:], 0.0)
         nc.scalar.activation(out=warm2[:], in_=warm[:], func=ACT.Exp)
+        nc.vector.memset(zz[:], 0.0)
+        nc.vector.memset(be3[:], 0.0)
         for r in range(2):
             nc.scalar.dma_start(out=be3[8 * r : 8 * r + 8, :], in_=be[:, :])
-        nc.vector.memset(zz[:], 0.0)
         nc.vector.memset(wsp[:], 0.0)
         make_identity(nc, ident_b[:])
         make_identity(nc, ident_f[:])

@@ -97,10 +97,11 @@ def tile_enhancedmathematicalreasoning_pa_kernel(tc, hidden_states, op_logits, W
             nc.sync.dma_start(out=hraw[:, t, :], in_=tokens_h[:, t, :])
         load_w(0, 0, NW, NDIM)
         load_w(0, 1, NW, NDIM)
-        for n0 in (0, NW):
-            for g in range(G):
-                load_w(1, g, n0, n0 + NW)
-        for e in range(2, E):
+        for e in (1, 2):
+            for n0 in (0, NW):
+                for g in range(G):
+                    load_w(e, g, n0, n0 + NW)
+        for e in range(3, E):
             for g in range(G):
                 load_w(e, g, 0, NDIM)
 

@@ -95,12 +95,13 @@ def tile_enhancedmathematicalreasoning_pa_kernel(tc, hidden_states, op_logits, W
         load_w(0, 1, 0, NW)
         for t in range(T):
             nc.sync.dma_start(out=hraw[:, t, :], in_=tokens_h[:, t, :])
-        load_w(0, 0, NW, NDIM)
         load_w(0, 1, NW, NDIM)
-        for e in (1, 2):
-            for n0 in (0, NW):
-                for g in range(G):
-                    load_w(e, g, n0, n0 + NW)
+        load_w(0, 0, NW, NDIM)
+        load_w(1, 1, 0, NW)
+        load_w(1, 0, 0, NW)
+        for e, n0 in ((1, NW), (2, 0), (2, NW)):
+            for g in range(G):
+                load_w(e, g, n0, n0 + NW)
         for e in range(3, E):
             for g in range(G):
                 load_w(e, g, 0, NDIM)

@@ -42,6 +42,7 @@ def tile_enhancedmathematicalreasoning_pa_kernel(tc, hidden_states, op_logits, W
         grp = ctx.enter_context(tc.tile_pool(name="grp", bufs=3))
         grg = ctx.enter_context(tc.tile_pool(name="grg", bufs=1))
         grh = ctx.enter_context(tc.tile_pool(name="grh", bufs=1))
+        grx = ctx.enter_context(tc.tile_pool(name="grx", bufs=1))
         cod = ctx.enter_context(tc.tile_pool(name="cod", bufs=3))
         psum = ctx.enter_context(tc.psum_pool(name="psum", bufs=6))
         psum_pi = ctx.enter_context(tc.psum_pool(name="psum_pi", bufs=2))
@@ -54,7 +55,9 @@ def tile_enhancedmathematicalreasoning_pa_kernel(tc, hidden_states, op_logits, W
             raw.append(raw_e)
         hraw = const.tile([P, T, KDIM], BF16, name="hraw")
         be3 = const.tile([P, NDIM], BF16, name="be3")
-        hg = const.tile([P, T, KDIM], BF16, name="hg", align_bytes=64)
+        hg_a = const.tile([P, 2 * KDIM], BF16, name="hg_a", align_bytes=64)
+        hg_b = grx.tile([P, 2 * KDIM], BF16, name="hg_b", tag="g1", align_bytes=64)
+        hg = [hg_a[:, 0:KDIM], hg_a[:, KDIM : 2 * KDIM], hg_b[:, 0:KDIM], hg_b[:, KDIM : 2 * KDIM]]
         hc = const.tile([P, T, KDIM // 4], U32, name="hc", align_bytes=64)
         hs = const.tile([P, T, KDIM // 4], U8, name="hs", align_bytes=64)
         acc = const.tile([P, T, NDIM], F32, name="acc")
@@ -142,7 +145,7 @@ def tile_enhancedmathematicalreasoning_pa_kernel(tc, hidden_states, op_logits, W
 
         def interleave_pass1(u):
             e, n0 = ORDER[u][0], ORDER[u][1] * NW
-            pool = grg if u < 2 else grh
+            pool = grx if u < 2 else grh
             g1 = pool.tile([P, 4 * NW], BF16, name="g1_%d" % u, tag="g1", align_bytes=64)
             pass1[u] = g1
             split = NW - XG
@@ -240,7 +243,7 @@ def tile_enhancedmathematicalreasoning_pa_kernel(tc, hidden_states, op_logits, W
             nc.vector.quantize_mx(
                 out=hc[:, t0:t1, :].rearrange("p t x -> p (t x)").bitcast(FP8X4),
                 scales=hs[:, t0:t1, :].rearrange("p t x -> p (t x)"),
-                in_=hg[:, t0:t1, :].rearrange("p t k -> p (t k)"),
+                in_=hg_a[:] if t1 - t0 == 2 else hg[t0],
             )
 
         for t in range(T):
@@ -256,7 +259,7 @@ def tile_enhancedmathematicalreasoning_pa_kernel(tc, hidden_states, op_logits, W
                 quantize_hidden(0, 2)
             copy_out = nc.scalar.copy if t < XS else nc.vector.tensor_copy
             copy_out(
-                out=hg[:, t, :].bitcast(F32).rearrange("p (g r u) -> p g r u", g=2, u=2),
+                out=hg[t].bitcast(F32).rearrange("p (g r u) -> p g r u", g=2, u=2),
                 in_=xt[:].rearrange("p (g u) r -> p g r u", u=2),
             )
 

@@ -96,8 +96,10 @@ def tile_enhancedmathematicalreasoning_pa_kernel(tc, hidden_states, op_logits, W
 
         load_w(0, 0, 0, NW)
         load_w(0, 1, 0, NW)
-        for t in range(T):
+        for t in range(T - 1):
             nc.sync.dma_start(out=hraw[:, t, :], in_=tokens_h[:, t, :])
+        for g in range(G):
+            nc.sync.dma_start(out=hraw[:, T - 1, 512 * g : 512 * (g + 1)], in_=tokens_h[:, T - 1, 512 * g : 512 * (g + 1)])
         load_w(0, 1, NW, NDIM)
         load_w(0, 0, NW, NDIM)
         load_w(1, 1, 0, NW)
@@ -246,7 +248,14 @@ def tile_enhancedmathematicalreasoning_pa_kernel(tc, hidden_states, op_logits, W
                 in_=hg_a[:] if t1 - t0 == 2 else hg[t0],
             )
 
-        for t in range(T):
+        def quantize_hidden_pass(t, g):
+            nc.vector.quantize_mx(
+                out=hc[:, t, g * P : (g + 1) * P].bitcast(FP8X4),
+                scales=hs[:, t, g * P : (g + 1) * P],
+                in_=hg[t][:, 512 * g : 512 * (g + 1)],
+            )
+
+        for t in range(T - 1):
             words = hraw[:, t, :].bitcast(F32)
             xt = psum.tile([P, 4, P], F32, name="xt%d" % t, tag="ps")
             for g in range(G):
@@ -254,13 +263,21 @@ def tile_enhancedmathematicalreasoning_pa_kernel(tc, hidden_states, op_logits, W
                     nc.tensor.transpose(
                         xt[:, 2 * g + u, :], words[:, 256 * g + u : 256 * (g + 1) : 2], ident_f[:]
                     )
-            if t == XS:
-                quantize(0)
-                quantize_hidden(0, 2)
-            copy_out = nc.scalar.copy if t < XS else nc.vector.tensor_copy
-            copy_out(
+            nc.scalar.copy(
                 out=hg[t].bitcast(F32).rearrange("p (g r u) -> p g r u", g=2, u=2),
                 in_=xt[:].rearrange("p (g u) r -> p g r u", u=2),
+            )
+        quantize(0)
+        quantize_hidden(0, 2)
+        words = hraw[:, T - 1, :].bitcast(F32)
+        for g in range(G):
+            xh = psum.tile([P, 2, P], F32, name="xh%d" % g, tag="ps")
+            for u in range(2):
+                nc.tensor.transpose(xh[:, u, :], words[:, 256 * g + u : 256 * (g + 1) : 2], ident_f[:])
+            copy_out = nc.vector.tensor_copy if g == 0 else nc.scalar.copy
+            copy_out(
+                out=hg[T - 1][:, 512 * g : 512 * (g + 1)].bitcast(F32).rearrange("p (r u) -> p r u", u=2),
+                in_=xh[:].rearrange("p u r -> p r u"),
             )
 
         pbs = {}
@@ -271,7 +288,8 @@ def tile_enhancedmathematicalreasoning_pa_kernel(tc, hidden_states, op_logits, W
                 out=pb[:], lhsT=wT[:, t, :], rhs=be3[:, nh * NW : (nh + 1) * NW], start=True, stop=True
             )
         quantize_hidden(2, 3)
-        quantize_hidden(3, 4)
+        quantize_hidden_pass(3, 0)
+        quantize_hidden_pass(3, 1)
         for t in range(T - 1):
             nc.scalar.activation(out=acc[:, t, 0:NW], in_=pbs[t][:], func=ACT.Copy, scale=rs[:, t : t + 1])
         nc.vector.tensor_scalar(

from contextlib import ExitStack

import concourse.mybir as mybir
from concourse.masks import make_identity

FLOPS = 2 * 512 * 1024 * 1024 * 8

F32 = mybir.dt.float32
BF16 = mybir.dt.bfloat16
U32 = mybir.dt.uint32
U8 = mybir.dt.uint8
FP8X4 = mybir.dt.float8_e4m3fn_x4
FP8 = mybir.dt.float8_e4m3fn
ALU = mybir.AluOpType
ACT = mybir.ActivationFunctionType
AX = mybir.AxisListType

P = 128
T = 4
E = 8
KDIM = 1024
NDIM = 1024
G = 2
NW = 512
UNITS = 16
Y_SCALE = 380.0
XP = 128
XG1 = 160
XS = 3
XG = 320


def tile_enhancedmathematicalreasoning_pa_kernel(tc, hidden_states, op_logits, We, be, out_0, out_1):
    nc = tc.nc
    tokens_h = hidden_states.flatten_outer_dims().rearrange("(p t) k -> p t k", t=T)
    tokens_l = op_logits.flatten_outer_dims().rearrange("(p t) e -> p t e", t=T)
    tokens_0 = out_0.flatten_outer_dims().rearrange("(p t) n -> p t n", t=T)
    tokens_1 = out_1.flatten_outer_dims().rearrange("(p t) n -> p t n", t=T)
    ORDER = [(e, nh) for e in range(6) for nh in range(2)] + [(6, 0), (7, 0), (6, 1), (7, 1)]
    with ExitStack() as ctx:
        const = ctx.enter_context(tc.tile_pool(name="const", bufs=1))
        grp = ctx.enter_context(tc.tile_pool(name="grp", bufs=3))
        grg = ctx.enter_context(tc.tile_pool(name="grg", bufs=1))
        grh = ctx.enter_context(tc.tile_pool(name="grh", bufs=1))
        grx = ctx.enter_context(tc.tile_pool(name="grx", bufs=1))
        cod = ctx.enter_context(tc.tile_pool(name="cod", bufs=3))
        psum = ctx.enter_context(tc.psum_pool(name="psum", bufs=6))
        psum_pi = ctx.enter_context(tc.psum_pool(name="psum_pi", bufs=2))
        ctx.enter_context(tc.manual_schedule())

        lg = const.tile([P, T, E], BF16, name="lg")
        raw = []
        for e in range(E):
            raw_e = const.tile([P, G, 4, NDIM], BF16, name="raw%d" % e)
            raw.append(raw_e)
        hraw = const.tile([P, T, KDIM], BF16, name="hraw")
        be3 = const.tile([P, NDIM], BF16, name="be3")
        hg_a = const.tile([P, 2 * KDIM], BF16, name="hg_a", align_bytes=64)
        hg_b = grx.tile([P, 2 * KDIM], BF16, name="hg_b", tag="g1", align_bytes=64)
        hg = [hg_a[:, 0:KDIM], hg_a[:, KDIM : 2 * KDIM], hg_b[:, 0:KDIM], hg_b[:, KDIM : 2 * KDIM]]
        hc = const.tile([P, T, KDIM // 4], U32, name="hc", align_bytes=64)
        hs = const.tile([P, T, KDIM // 4], U8, name="hs", align_bytes=64)
        acc = const.tile([P, T, NDIM], F32, name="acc")
        o8 = const.tile([P, T, NDIM], FP8, name="o8")
        ident_f = const.tile([P, P], F32, name="ident_f")
        ident_b = const.tile([P, P], BF16, name="ident_b")
        wsp = const.tile([P, T, P], BF16, name="wsp")
        wT = const.tile([P, T, P], BF16, name="wT")
        warm = const.tile([P, 1], F32, name="warm")
        warm2 = const.tile([P, 1], F32, name="warm2")
        mx = const.tile([P, T], F32, name="mx")
        dl = const.tile([P, T, E], F32, name="dl")
        sm = const.tile([P, T], F32, name="sm")
        rs = const.tile([P, T], F32, name="rs")
        ex = const.tile([P, T, E], F32, name="ex")
        w = const.tile([P, T, E], F32, name="w")
        r1 = const.tile([P, T, E], F32, name="r1")
        zz = const.tile([P, NW], BF16, name="zz")

        def load_w(e, g, n0, n1):
            nc.sync.dma_start(
                out=raw[e][:, g, :, n0:n1],
                in_=We[e, g * 512 : (g + 1) * 512, n0:n1].rearrange("(p j) n -> p j n", j=4),
            )

        nc.scalar.dma_start(out=lg[:], in_=tokens_l)
        nc.vector.memset(warm[:], 0.0)
        nc.scalar.activation(out=warm2[:], in_=warm[:], func=ACT.Exp)
        nc.vector.memset(zz[:], 0.0)
        nc.vector.memset(be3[:], 0.0)
        for r in range(2):
            nc.scalar.dma_start(out=be3[8 * r : 8 * r + 8, :], in_=be[:, :])
        nc.vector.memset(wsp[:], 0.0)
        make_identity(nc, ident_b[:])
        make_identity(nc, ident_f[:])

        load_w(0, 0, 0, NW)
        load_w(0, 1, 0, NW)
        for t in range(T - 1):
            nc.sync.dma_start(out=hraw[:, t, :], in_=tokens_h[:, t, :])
        for g in range(G):
            nc.sync.dma_start(out=hraw[:, T - 1, 512 * g : 512 * (g + 1)], in_=tokens_h[:, T - 1, 512 * g : 512 * (g + 1)])
        load_w(0, 1, NW, NDIM)
        load_w(0, 0, NW, NDIM)
        load_w(1, 1, 0, NW)
        load_w(1, 0, 0, NW)
        for e, n0 in ((1, NW), (2, 0), (2, NW)):
            for g in range(G):
                load_w(e, g, n0, n0 + NW)
        for e in range(3, E):
            for g in range(G):
                load_w(e, g, 0, NDIM)

        pass0 = {}
        pass1 = {}
        codes = {}
        scales = {}
        banks = {}

        def rows_to_words(dst, src):
            return dst.rearrange("p (c j) -> p c j", j=4), src.rearrange("p j c -> p c j")

        def interleave_pass0(u, gpsimd_cols=0):
            e, n0 = ORDER[u][0], ORDER[u][1] * NW
            g0 = grp.tile([P, 4 * NW], BF16, name="g0_%d" % u, tag="g0", align_bytes=64)
            pass0[u] = g0
            split = NW - XP
            pi = psum_pi.tile([P, 4 * XP], BF16, name="pi%d" % u, tag="pi")
            for c0 in range(0, XP, P):
                nc.tensor.matmul(
                    out=pi[:, 4 * c0 : 4 * (c0 + P)],
                    lhsT=ident_b[:],
                    rhs=raw[e][:, 0, :, n0 + split + c0 : n0 + split + c0 + P].rearrange("p j c -> p c j"),
                    start=True,
                    stop=True,
                )
            mine = split - gpsimd_cols
            dst, src = rows_to_words(g0[:, 0 : 4 * mine], raw[e][:, 0, :, n0 : n0 + mine])
            nc.scalar.copy(out=dst, in_=src)
            nc.scalar.copy(out=g0[:, 4 * split : 4 * NW], in_=pi[:])

        def interleave_pass0_gpsimd(u, gpsimd_cols):
            e, n0 = ORDER[u][0], ORDER[u][1] * NW
            c0, c1 = NW - XP - gpsimd_cols, NW - XP
            dst, src = rows_to_words(pass0[u][:, 4 * c0 : 4 * c1], raw[e][:, 0, :, n0 + c0 : n0 + c1])
            nc.gpsimd.tensor_scalar(out=dst, in0=src, scalar1=1.0, scalar2=0.0, op0=ALU.mult, op1=ALU.add)

        def interleave_pass1(u):
            e, n0 = ORDER[u][0], ORDER[u][1] * NW
            pool = grx if u < 2 else grh
            g1 = pool.tile([P, 4 * NW], BF16, name="g1_%d" % u, tag="g1", align_bytes=64)
            pass1[u] = g1
            split = NW - XG
            dst, src = rows_to_words(g1[:, 0 : 4 * split], raw[e][:, 1, :, n0 : n0 + split])
            nc.scalar.copy(out=dst, in_=src)
            dst, src = rows_to_words(g1[:, 4 * split : 4 * NW], raw[e][:, 1, :, n0 + split : n0 + NW])
            nc.gpsimd.tensor_scalar(out=dst, in0=src, scalar1=1.0, scalar2=0.0, op0=ALU.mult, op1=ALU.add)

        def interleave_pass1_vector(u):
            e, n0 = ORDER[u][0], ORDER[u][1] * NW
            g1 = grg.tile([P, 4 * NW], BF16, name="g1_%d" % u, tag="g1", align_bytes=64)
            pass1[u] = g1
            dst, src = rows_to_words(g1[:], raw[e][:, 1, :, n0 : n0 + NW])
            nc.vector.tensor_copy(out=dst, in_=src)

        def quantize_pass0(u):
            ct = cod.tile([P, G * NW], U32, name="ct%d" % u, tag="ct", align_bytes=64)
            sc = cod.tile([P, G * NW], U8, name="sc%d" % u, tag="sc", align_bytes=64)
            codes[u] = ct
            scales[u] = sc
            nc.vector.quantize_mx(out=ct[:, 0:NW].bitcast(FP8X4), scales=sc[:, 0:NW], in_=pass0[u][:])

        def quantize_pass1(u):
            nc.vector.quantize_mx(
                out=codes[u][:, NW : 2 * NW].bitcast(FP8X4), scales=scales[u][:, NW : 2 * NW], in_=pass1[u][:]
            )

        def quantize(u):
            quantize_pass0(u)
            quantize_pass1(u)

        def multiply(u):
            banks[u] = []
            for t in range(T):
                ps = psum.tile([P, NW], F32, name="ps%d_%d" % (u, t), tag="ps")
                banks[u].append(ps)
                for g in range(G):
                    nc.tensor.matmul_mx(
                        out=ps[:],
                        lhsT=hc[:, t, g * P : (g + 1) * P].bitcast(FP8X4),
                        lhsT_scale=hs[:, t, g * P : (g + 1) * P],
                        rhs=codes[u][:, g * NW : (g + 1) * NW].bitcast(FP8X4),
                        rhs_scale=scales[u][:, g * NW : (g + 1) * NW],
                        start=(g == 0),
                        stop=(g == G - 1),
                    )

        def accumulate_tile(u, t, pieces=1):
            e, nh = ORDER[u]
            width = NW // pieces
            for i in range(pieces):
                cols = slice(nh * NW + i * width, nh * NW + (i + 1) * width)
                nc.vector.scalar_tensor_tensor(
                    out=acc[:, t, cols], in0=banks[u][t][:, i * width : (i + 1) * width], scalar=w[:, t, e : e + 1],
                    in1=acc[:, t, cols], op0=ALU.mult, op1=ALU.add,
                )
                if e == E - 1:
                    nc.sync.dma_start(out=tokens_0[:, t, cols], in_=acc[:, t, cols])
                    nc.scalar.activation(
                        out=o8[:, t, cols], in_=acc[:, t, cols], func=ACT.Copy, scale=Y_SCALE, saturate=False
                    )
                    nc.sync.dma_start(out=tokens_1[:, t, cols], in_=o8[:, t, cols].bitcast(U8))

        def accumulate(u):
            for t in range(T):
                accumulate_tile(u, t)

        dm = psum.tile([P, NW], F32, name="dm", tag="ps")

        def keep_busy(n, rhs):
            for i in range(n):
                nc.tensor.matmul(out=dm[:], lhsT=ident_b[:], rhs=rhs, start=True, stop=True)

        keep_busy(7, zz[:])

        nc.vector.tensor_reduce(out=mx[:], in_=lg[:], axis=AX.X, op=ALU.max)
        nc.vector.tensor_tensor(out=dl[:], in0=lg[:], in1=mx[:].unsqueeze(2).to_broadcast([P, T, E]), op=ALU.subtract)
        nc.scalar.activation(out=ex[:], in_=dl[:], func=ACT.Exp)
        interleave_pass0(0)
        keep_busy(2, raw[0][:, 0, 0, 0:NW])
        nc.vector.tensor_copy(out=wsp[:, :, 0:8], in_=ex[:])
        nc.vector.tensor_reduce(out=sm[:], in_=ex[:], axis=AX.X, op=ALU.add)
        nc.vector.tensor_tensor(out=r1[:], in0=ex[:], in1=wsp[:, :, 0:8], op=ALU.subtract)
        nc.vector.reciprocal(out=rs[:], in_=sm[:])
        nc.vector.tensor_copy(out=wsp[:, :, 8:16], in_=r1[:])
        nc.vector.tensor_tensor(out=w[:], in0=ex[:], in1=rs[:].unsqueeze(2).to_broadcast([P, T, E]), op=ALU.mult)
        interleave_pass1_vector(0)
        pw = psum.tile([P, T, P], BF16, name="pw", tag="ps")
        for t in range(T):
            nc.tensor.transpose(pw[:, t, :], wsp[:, t, :], ident_b[:])
        nc.vector.tensor_copy(out=wT[:], in_=pw[:])
        keep_busy(2, raw[0][:, 1, 0, 0:NW])

        def quantize_hidden(t0, t1):
            nc.vector.quantize_mx(
                out=hc[:, t0:t1, :].rearrange("p t x -> p (t x)").bitcast(FP8X4),
                scales=hs[:, t0:t1, :].rearrange("p t x -> p (t x)"),
                in_=hg_a[:] if t1 - t0 == 2 else hg[t0],
            )

        def quantize_hidden_pass(t, g):
            nc.vector.quantize_mx(
                out=hc[:, t, g * P : (g + 1) * P].bitcast(FP8X4),
                scales=hs[:, t, g * P : (g + 1) * P],
                in_=hg[t][:, 512 * g : 512 * (g + 1)],
            )

        for t in range(T - 1):
            words = hraw[:, t, :].bitcast(F32)
            xt = psum.tile([P, 4, P], F32, name="xt%d" % t, tag="ps")
            for g in range(G):
                for u in range(2):
                    nc.tensor.transpose(
                        xt[:, 2 * g + u, :], words[:, 256 * g + u : 256 * (g + 1) : 2], ident_f[:]
                    )
            nc.scalar.copy(
                out=hg[t].bitcast(F32).rearrange("p (g r u) -> p g r u", g=2, u=2),
                in_=xt[:].rearrange("p (g u) r -> p g r u", u=2),
            )
        quantize(0)
        quantize_hidden(0, 2)
        words = hraw[:, T - 1, :].bitcast(F32)
        for g in range(G):
            xh = psum.tile([P, 2, P], F32, name="xh%d" % g, tag="ps")
            for u in range(2):
                nc.tensor.transpose(xh[:, u, :], words[:, 256 * g + u : 256 * (g + 1) : 2], ident_f[:])
            copy_out = nc.vector.tensor_copy if g == 0 else nc.scalar.copy
            copy_out(
                out=hg[T - 1][:, 512 * g : 512 * (g + 1)].bitcast(F32).rearrange("p (r u) -> p r u", u=2),
                in_=xh[:].rearrange("p u r -> p r u"),
            )

        pbs = {}
        for nh, t in [(0, 0), (0, 3), (0, 1), (1, 0), (0, 2), (1, 1), (1, 2), (1, 3)]:
            pb = psum.tile([P, NW], F32, name="pb%d_%d" % (nh, t), tag="ps")
            pbs[T * nh + t] = pb
            nc.tensor.matmul(
                out=pb[:], lhsT=wT[:, t, :], rhs=be3[:, nh * NW : (nh + 1) * NW], start=True, stop=True
            )
        quantize_hidden(2, 3)
        quantize_hidden_pass(3, 0)
        quantize_hidden_pass(3, 1)
        for t in range(T - 1):
            nc.scalar.activation(out=acc[:, t, 0:NW], in_=pbs[t][:], func=ACT.Copy, scale=rs[:, t : t + 1])
        nc.vector.tensor_scalar(
            out=acc[:, T - 1, 0:NW], in0=pbs[T - 1][:], scalar1=rs[:, T - 1 : T], scalar2=None, op0=ALU.mult
        )
        interleave_pass0(1, gpsimd_cols=XG1)
        multiply(0)
        interleave_pass1(1)
        interleave_pass0_gpsimd(1, XG1)
        for t in range(T):
            nc.vector.tensor_scalar(
                out=acc[:, t, NW:NDIM], in0=pbs[T + t][:], scalar1=rs[:, t : t + 1], scalar2=None, op0=ALU.mult
            )
        interleave_pass0(2)
        interleave_pass1(2)
        interleave_pass0(3)
        accumulate(0)
        quantize(1)
        multiply(1)
        quantize(2)
        multiply(2)

        for u in range(3, UNITS):
            interleave_pass1(u)
            if u + 1 < UNITS:
                interleave_pass0(u + 1)
            accumulate(u - 2)
            quantize(u)
            multiply(u)
        a, b = UNITS - 2, UNITS - 1
        e_a, nh_a = ORDER[a]
        side = grh.tile([P, NW], F32, name="side", tag="g1", align_bytes=64)
        nc.scalar.activation(out=side[:], in_=banks[a][T - 1][:], func=ACT.Copy, scale=w[:, T - 1, e_a : e_a + 1])
        last_cols = slice(nh_a * NW, (nh_a + 1) * NW)
        nc.gpsimd.tensor_tensor(out=acc[:, T - 1, last_cols], in0=acc[:, T - 1, last_cols], in1=side[:], op=ALU.add)
        accumulate_tile(a, 0)
        accumulate_tile(a, 1)
        accumulate_tile(b, 0)
        accumulate_tile(a, 2)
        accumulate_tile(b, 1)
        accumulate_tile(b, 2)
        accumulate_tile(b, 3, pieces=2)
